import numpy as np
import ml_dtypes


def mxq(x, axis, fmt="e4m3"):
    dtype, down = {"e4m3": (ml_dtypes.float8_e4m3fn, 7), "e5m2": (ml_dtypes.float8_e5m2, 14)}[fmt]
    v = np.moveaxis(np.asarray(x, np.float32).astype(ml_dtypes.bfloat16).astype(np.float64), axis, -1)
    blocks = v.reshape(v.shape[:-1] + (-1, 32))
    amax = np.abs(blocks).max(-1, keepdims=True)
    byte = np.maximum(np.where(amax > 0, np.frexp(amax)[1] - 1 + 127, 0) - down, 1)
    scale = np.exp2(byte - 127.0)
    codes = (blocks / scale).astype(np.float32).astype(dtype).astype(np.float64)
    return np.moveaxis((codes * scale).reshape(v.shape), -1, axis)


WIDE = False


def mx_kscale(k):
    if not WIDE:
        return np.ones(k)
    levels = np.array([10, -10, 5, -5, 0])
    if k % 512:
        return np.exp2(np.random.permutation(np.resize(levels, k // 32))).repeat(32)
    a = np.empty((k // 512, 16))
    for p in range(k // 512):
        a[p, :8] = np.random.permutation(np.resize(levels, 8))
        for g in range(8):
            far = levels[np.abs(levels - a[p, g]) >= 10]
            a[p, g + 8] = far[np.random.randint(len(far))]
    return np.exp2(a.ravel()).repeat(32)


BF16 = ml_dtypes.bfloat16


def bf(x):
    return np.asarray(x, np.float32).astype(BF16)


def f64(x):
    return np.asarray(x).astype(np.float64)


N, K, F, H, O, Q, GS, SO = 128, 16, 512, 1024, 1024, 1024, 3, 2


def setup_inputs():
    s, t = mx_kscale(F), mx_kscale(H)
    return {"x": bf(np.random.standard_normal((N, F)) * s),
            "contexts": bf(np.random.standard_normal((N, K, F)) * s),
            "attn": bf(np.random.random((N, K))),
            "Wn": bf(np.random.standard_normal((H, F)) * 0.5 / np.sqrt(F) / s * t[:, None]),
            "bn": bf(np.random.standard_normal(H) * 0.1 * t),
            "Wc": bf(np.random.standard_normal((H, F)) * 1.5 / np.sqrt(F) / s * t[:, None]),
            "bc": bf(np.random.standard_normal(H) * 0.1 * t),
            "Wu": bf(np.random.standard_normal((O, H)) * 1.5 / np.sqrt(H) / t),
            "bu": bf(np.random.standard_normal(O) * 0.1)}


def reference(x, contexts, attn, Wn, bn, Wc, bc, Wu, bu):
    xt = (mxq(f64(x), 1, "e4m3") @ mxq(f64(Wn).T, 0, "e4m3")) + f64(bn)
    ct = (mxq(f64(contexts).reshape(N * K, F), 1, "e4m3") @ mxq(f64(Wc).T, 0, "e4m3")).reshape(N, K, H) + f64(bc)
    ca = (ct * f64(attn)[..., None]).mean(axis=1)
    return (mxq(xt + ca, 1, "e4m3") @ mxq(f64(Wu).T, 0, "e4m3")) + f64(bu)

@@ -1,0 +1,267 @@
+from contextlib import ExitStack
+
+import concourse.mybir as mybir
+from concourse.masks import make_identity
+
+F32 = mybir.dt.float32
+BF16 = mybir.dt.bfloat16
+U32 = mybir.dt.uint32
+U8 = mybir.dt.uint8
+FP8X4 = mybir.dt.float8_e4m3fn_x4
+MULT = mybir.AluOpType.mult
+ADD = mybir.AluOpType.add
+COPY = mybir.ActivationFunctionType.Copy
+
+P = 128
+PACK = 4
+K_PASS = P * PACK
+BANK = 512
+
+NODES = 128
+CONTEXTS = 16
+F_IN = 512
+HIDDEN = 1024
+F_OUT = 1024
+HALVES = HIDDEN // K_PASS
+SIDES = F_OUT // BANK
+
+GROUP = 4
+PAIR = 2
+PREPARED_PER_ROUND = (2, 1)
+SCALAR_EVERY = 6
+
+FLOPS = 2 * (NODES * F_IN * HIDDEN + NODES * CONTEXTS * F_IN * HIDDEN + NODES * HIDDEN * F_OUT)
+
+
+def tile_nodeembeddinglayer_pa_kernel(tc, x, contexts, attn, Wn, bn, Wc, bc, Wu, bu, out):
+    nc = tc.nc
+    with ExitStack() as stack:
+        stack.enter_context(tc.manual_schedule())
+        keep = stack.enter_context(tc.tile_pool(name="keep", bufs=1))
+        turned_pool = stack.enter_context(tc.psum_pool(name="turned_pool", bufs=4))
+        product_pool = stack.enter_context(tc.psum_pool(name="product_pool", bufs=4))
+
+        attn_raw = keep.tile([P, CONTEXTS], BF16, name="attn_raw")
+        nc.scalar.dma_start(out=attn_raw[:], in_=attn)
+        bias_rows = keep.tile([P, HIDDEN], BF16, name="bias_rows")
+        nc.vector.memset(bias_rows[:], 0.0)
+        nc.scalar.dma_start(out=bias_rows[0:CONTEXTS, :], in_=bc.partition_broadcast(CONTEXTS))
+        nc.scalar.dma_start(out=bias_rows[CONTEXTS : CONTEXTS + 1, :], in_=bn.unsqueeze(0))
+
+        wc_raw = keep.tile([P, HALVES * GROUP * F_IN], BF16, name="wc_raw")
+        wn_raw = keep.tile([P, HALVES * GROUP * F_IN], BF16, name="wn_raw")
+        ctx_raw = keep.tile([P, CONTEXTS * F_IN], BF16, name="ctx_raw")
+        x_raw = keep.tile([P, F_IN], BF16, name="x_raw")
+        wu_raw = keep.tile([P, SIDES * GROUP * HIDDEN], BF16, name="wu_raw")
+        bu_rows = keep.tile([P, F_OUT], BF16, name="bu_rows")
+
+        def load_hidden_rows(raw, weight, half):
+            rows = weight.rearrange("(g p t) f -> g p (t f)", g=HALVES, t=PACK)[half]
+            for u in range(2):
+                pair = half * 2 + u
+                nc.sync.dma_start(
+                    out=raw[:, pair * PAIR * F_IN : (pair + 1) * PAIR * F_IN],
+                    in_=rows[:, u * PAIR * F_IN : (u + 1) * PAIR * F_IN],
+                )
+
+        def load_contexts(pair):
+            columns = slice(pair * PAIR * F_IN, (pair + 1) * PAIR * F_IN)
+            nc.sync.dma_start(out=ctx_raw[:, columns], in_=contexts.rearrange("n k f -> n (k f)")[:, columns])
+
+        def load_output_rows(pair):
+            nc.sync.dma_start(
+                out=wu_raw[:, pair * PAIR * HIDDEN : (pair + 1) * PAIR * HIDDEN].rearrange(
+                    "p (b h) -> p b h", b=PAIR
+                ),
+                in_=Wu.rearrange("(b p) h -> p b h", p=P)[:, pair * PAIR : (pair + 1) * PAIR, :],
+            )
+
+        load_hidden_rows(wc_raw, Wc, 0)
+        for pair in range(CONTEXTS // PAIR):
+            load_contexts(pair)
+        nc.sync.dma_start(out=x_raw[:], in_=x)
+        load_hidden_rows(wn_raw, Wn, 0)
+        load_hidden_rows(wc_raw, Wc, 1)
+        load_hidden_rows(wn_raw, Wn, 1)
+        for pair in range(SIDES * GROUP // PAIR):
+            load_output_rows(pair)
+        nc.sync.dma_start(out=bu_rows[:], in_=bu.partition_broadcast(P))
+
+        identity_words = keep.tile([P, P], F32, name="identity_words")
+        make_identity(nc, identity_words[:])
+        identity_values = keep.tile([P, P], BF16, name="identity_values")
+        make_identity(nc, identity_values[:])
+
+        def new_operand(name, blocks, source):
+            columns = blocks * P
+            return {
+                "blocks": blocks,
+                "source": source,
+                "grouped": keep.tile([P, columns * PACK], BF16, name=name + "_grouped", align_bytes=64),
+                "codes": keep.tile([P, columns], U32, name=name + "_codes", align_bytes=64),
+                "scales": keep.tile([P, columns], U8, name=name + "_scales", align_bytes=64),
+            }
+
+        def pairs_of(operand):
+            step = min(operand["blocks"], PAIR)
+            return [(operand, first, step) for first in range(0, operand["blocks"], step)]
+
+        def words(raw, blocks):
+            return raw[:].bitcast(F32).rearrange("p (b w) -> p b w", b=blocks)
+
+        def turn(piece, copy_out):
+            operand, first, count = piece
+            turned = turned_pool.tile([P, count, 2, P], F32, tag="turned")
+            for i in range(count):
+                for u in range(2):
+                    nc.tensor.transpose(
+                        turned[:, i, u, :], operand["source"][:, first + i, u : 2 * P : 2], identity_words[:]
+                    )
+            copy_out(
+                out=operand["grouped"][:].bitcast(F32)[:, first * P * 2 : (first + count) * P * 2].rearrange(
+                    "p (i r u) -> p i r u", i=count, u=2
+                ),
+                in_=turned[:].rearrange("p i u r -> p i r u"),
+            )
+
+        def quantise(piece):
+            operand, first, count = piece
+            columns = slice(first * P, (first + count) * P)
+            nc.vector.quantize_mx(
+                out=operand["codes"][:, columns].bitcast(FP8X4),
+                scales=operand["scales"][:, columns],
+                in_=operand["grouped"][:, first * P * PACK : (first + count) * P * PACK],
+            )
+
+        def mx_pass(acc, stationary, block, moving, start, stop):
+            columns = slice(block * P, (block + 1) * P)
+            nc.tensor.matmul_mx(
+                out=acc[:],
+                lhsT=stationary["codes"][:, columns].bitcast(FP8X4),
+                lhsT_scale=stationary["scales"][:, columns],
+                rhs=moving["codes"][:].bitcast(FP8X4),
+                rhs_scale=moving["scales"][:],
+                start=start,
+                stop=stop,
+            )
+
+        wc_words = words(wc_raw, HALVES * GROUP)
+        wn_words = words(wn_raw, HALVES * GROUP)
+        wu_words = words(wu_raw, SIDES * GROUP)
+
+        ctx_op = new_operand("ctx", CONTEXTS, words(ctx_raw, CONTEXTS))
+        x_op = new_operand("x", 1, words(x_raw, 1))
+        wc_ops = [new_operand("wc%d" % g, GROUP, wc_words[:, g * GROUP : (g + 1) * GROUP, :]) for g in range(HALVES)]
+        wn_ops = [new_operand("wn%d" % g, GROUP, wn_words[:, g * GROUP : (g + 1) * GROUP, :]) for g in range(HALVES)]
+        h_ops = [new_operand("h%d" % g, 1, None) for g in range(HALVES)]
+        wu_ops = [
+            [
+                new_operand(
+                    "wu%d%d" % (g, side),
+                    GROUP,
+                    wu_words[:, side * GROUP : (side + 1) * GROUP, g * K_PASS // 2 : (g + 1) * K_PASS // 2],
+                )
+                for side in range(SIDES)
+            ]
+            for g in range(HALVES)
+        ]
+
+        mean_weights = keep.tile([P, CONTEXTS], F32, name="mean_weights")
+        nc.scalar.activation(out=mean_weights[:], in_=attn_raw[:], func=COPY, scale=1.0 / CONTEXTS)
+        bias_weights = keep.tile([P, P], BF16, name="bias_weights")
+        nc.vector.memset(bias_weights[:], 0.0)
+        nc.vector.memset(bias_weights[:, CONTEXTS : CONTEXTS + 1], 1.0)
+        nc.vector.tensor_copy(out=bias_weights[:, 0:CONTEXTS], in_=mean_weights[:])
+
+        waiting = (
+            pairs_of(wc_ops[0]) + pairs_of(ctx_op) + pairs_of(x_op) + pairs_of(wn_ops[0]) + pairs_of(wc_ops[1])
+            + pairs_of(wn_ops[1]) + pairs_of(wu_ops[0][0]) + pairs_of(wu_ops[0][1])
+        )
+        waiting_late = pairs_of(wu_ops[1][0]) + pairs_of(wu_ops[1][1])
+
+        first_pieces, waiting = waiting[:4], waiting[4:]
+        turn(first_pieces[0], nc.scalar.copy)
+        turn(first_pieces[1], nc.vector.tensor_copy)
+        turn(first_pieces[2], nc.scalar.copy)
+        turn(first_pieces[3], nc.scalar.copy)
+        for piece in first_pieces:
+            quantise(piece)
+        turned_last_round, waiting = waiting[:1], waiting[1:]
+        turn(turned_last_round[0], nc.scalar.copy)
+        bias_turned = turned_pool.tile([P, P], BF16, tag="turned")
+        nc.tensor.transpose(bias_turned[:], bias_weights[:], identity_values[:])
+        bias_weights_t = keep.tile([P, P], BF16, name="bias_weights_t")
+        nc.scalar.copy(out=bias_weights_t[:], in_=bias_turned[:])
+
+        parts = []
+        rounds = 0
+        for half in range(HALVES):
+            terms = [(ctx_op, k, wc_ops[half], mean_weights[:, k : k + 1]) for k in range(CONTEXTS)]
+            terms.append((x_op, 0, wn_ops[half], 1.0))
+            sums = [keep.tile([P, BANK], F32, name="sum%d_%d" % (half, c)) for c in range(2)]
+            in_sums = 0
+            alone = []
+            for first in range(0, len(terms), PAIR):
+                for index in range(first, min(first + PAIR, len(terms))):
+                    stationary, block, moving, weight = terms[index]
+                    product = product_pool.tile([P, BANK], F32, tag="product")
+                    mx_pass(product, stationary, block, moving, True, True)
+                    if index % SCALAR_EVERY == SCALAR_EVERY - 1:
+                        weighted = keep.tile([P, BANK], F32, name="weighted%d_%d" % (half, index))
+                        nc.scalar.activation(out=weighted[:], in_=product[:], func=COPY, scale=weight)
+                        alone.append(weighted)
+                    elif in_sums < 2:
+                        nc.scalar.activation(out=sums[in_sums][:], in_=product[:], func=COPY, scale=weight)
+                        in_sums += 1
+                    else:
+                        running = sums[in_sums % 2]
+                        nc.vector.scalar_tensor_tensor(
+                            out=running[:], in0=product[:], scalar=weight, in1=running[:], op0=MULT, op1=ADD
+                        )
+                        in_sums += 1
+                for piece in turned_last_round:
+                    quantise(piece)
+                prepared = PREPARED_PER_ROUND[rounds % 2]
+                rounds += 1
+                turned_last_round, waiting = waiting[:prepared], waiting[prepared:]
+                spare = prepared - len(turned_last_round)
+                only_turned, waiting_late = waiting_late[:spare], waiting_late[spare:]
+                for piece in turned_last_round + only_turned:
+                    turn(piece, nc.scalar.copy)
+            parts.append(alone + [sums[in_sums % 2], sums[(in_sums - 1) % 2]])
+
+        bias_columns = bias_rows[:].rearrange("r (g p t) -> r g t p", g=HALVES, t=PACK)
+        for half in range(HALVES):
+            h_turned = turned_pool.tile([P, PACK, P], F32, tag="turned")
+            for t in range(PACK):
+                nc.tensor.matmul(
+                    out=h_turned[:, t, :], lhsT=bias_columns[:, half, t, :], rhs=bias_weights_t[:],
+                    start=(t == 0), stop=False,
+                )
+            for part in parts[half]:
+                for t in range(PACK):
+                    nc.tensor.matmul(
+                        out=h_turned[:, t, :], lhsT=part[:, t * P : (t + 1) * P], rhs=identity_words[:],
+                        is_transpose=True, start=False, stop=(part is parts[half][-1] and t == PACK - 1),
+                    )
+            nc.scalar.copy(
+                out=h_ops[half]["grouped"][:].rearrange("p (r t) -> p r t", t=PACK),
+                in_=h_turned[:].rearrange("p t r -> p r t"),
+            )
+
+        quantise(pairs_of(h_ops[0])[0])
+        out_sums = []
+        for side in range(SIDES):
+            out_sum = product_pool.tile([P, BANK], F32, tag="product")
+            mx_pass(out_sum, h_ops[0], 0, wu_ops[0][side], True, False)
+            out_sums.append(out_sum)
+        for side in range(SIDES):
+            for piece in pairs_of(wu_ops[1][side]):
+                quantise(piece)
+        quantise(pairs_of(h_ops[1])[0])
+        result = keep.tile([P, F_OUT], F32, name="result")
+        for side in range(SIDES):
+            columns = slice(side * BANK, (side + 1) * BANK)
+            mx_pass(out_sums[side], h_ops[1], 0, wu_ops[1][side], False, True)
+            nc.vector.tensor_add(out=result[:, columns], in0=out_sums[side][:], in1=bu_rows[:, columns])
+            nc.sync.dma_start(out=out[:, columns], in_=result[:, columns])

@@ -27,8 +27,13 @@ SIDES = F_OUT // BANK
 
 GROUP = 4
 PAIR = 2
-PREPARED_PER_ROUND = (2, 1)
-SCALAR_EVERY = 6
+ROUND = 5
+HEAD = 6
+ROUNDS = 7
+RUNS = (0, 3, 4, 3, 3, 3, 3)
+BIAS_ROUND = 3
+H_ROUND = 5
+LEFT_TO_SCALAR = ((11,), (11, 14))
 
 FLOPS = 2 * (NODES * F_IN * HIDDEN + NODES * CONTEXTS * F_IN * HIDDEN + NODES * HIDDEN * F_OUT)
 
@@ -38,8 +43,12 @@ def tile_nodeembeddinglayer_pa_kernel(tc, x, contexts, attn, Wn, bn, Wc, bc, Wu,
     with ExitStack() as stack:
         stack.enter_context(tc.manual_schedule())
         keep = stack.enter_context(tc.tile_pool(name="keep", bufs=1))
-        turned_pool = stack.enter_context(tc.psum_pool(name="turned_pool", bufs=4))
-        product_pool = stack.enter_context(tc.psum_pool(name="product_pool", bufs=4))
+        turned_pool = stack.enter_context(tc.psum_pool(name="turned_pool", bufs=3))
+        product_pool = stack.enter_context(tc.psum_pool(name="product_pool", bufs=5))
+
+        spark = keep.tile([P, 1], F32, name="spark")
+        nc.vector.memset(spark[:], 0.0)
+        nc.scalar.activation(out=spark[:], in_=spark[:], func=COPY, scale=1.0)
 
         attn_raw = keep.tile([P, CONTEXTS], BF16, name="attn_raw")
         nc.scalar.dma_start(out=attn_raw[:], in_=attn)
@@ -173,91 +182,98 @@ def tile_nodeembeddinglayer_pa_kernel(tc, x, contexts, attn, Wn, bn, Wc, bc, Wu,
         nc.vector.memset(bias_weights[:, CONTEXTS : CONTEXTS + 1], 1.0)
         nc.vector.tensor_copy(out=bias_weights[:, 0:CONTEXTS], in_=mean_weights[:])
 
-        waiting = (
+        pieces = (
             pairs_of(wc_ops[0]) + pairs_of(ctx_op) + pairs_of(x_op) + pairs_of(wn_ops[0]) + pairs_of(wc_ops[1])
-            + pairs_of(wn_ops[1]) + pairs_of(wu_ops[0][0]) + pairs_of(wu_ops[0][1])
+            + pairs_of(wn_ops[1]) + pairs_of(wu_ops[0][0]) + pairs_of(wu_ops[0][1]) + pairs_of(wu_ops[1][0])
+            + pairs_of(wu_ops[1][1])
         )
-        waiting_late = pairs_of(wu_ops[1][0]) + pairs_of(wu_ops[1][1])
 
-        first_pieces, waiting = waiting[:4], waiting[4:]
-        turn(first_pieces[0], nc.scalar.copy)
-        turn(first_pieces[1], nc.vector.tensor_copy)
-        turn(first_pieces[2], nc.scalar.copy)
-        turn(first_pieces[3], nc.scalar.copy)
-        for piece in first_pieces:
-            quantise(piece)
-        turned_last_round, waiting = waiting[:1], waiting[1:]
-        turn(turned_last_round[0], nc.scalar.copy)
-        bias_turned = turned_pool.tile([P, P], BF16, tag="turned")
-        nc.tensor.transpose(bias_turned[:], bias_weights[:], identity_values[:])
-        bias_weights_t = keep.tile([P, P], BF16, name="bias_weights_t")
-        nc.scalar.copy(out=bias_weights_t[:], in_=bias_turned[:])
+        for i in range(HEAD):
+            turn(pieces[i], nc.vector.tensor_copy if i % 3 == 1 else nc.scalar.copy)
+            if i > 0:
+                quantise(pieces[i - 1])
+        late = [pieces[HEAD - 1]]
+        done = HEAD
 
-        parts = []
-        rounds = 0
+        terms = []
         for half in range(HALVES):
-            terms = [(ctx_op, k, wc_ops[half], mean_weights[:, k : k + 1]) for k in range(CONTEXTS)]
-            terms.append((x_op, 0, wn_ops[half], 1.0))
-            sums = [keep.tile([P, BANK], F32, name="sum%d_%d" % (half, c)) for c in range(2)]
-            in_sums = 0
-            alone = []
-            for first in range(0, len(terms), PAIR):
-                for index in range(first, min(first + PAIR, len(terms))):
-                    stationary, block, moving, weight = terms[index]
-                    product = product_pool.tile([P, BANK], F32, tag="product")
-                    mx_pass(product, stationary, block, moving, True, True)
-                    if index % SCALAR_EVERY == SCALAR_EVERY - 1:
-                        weighted = keep.tile([P, BANK], F32, name="weighted%d_%d" % (half, index))
-                        nc.scalar.activation(out=weighted[:], in_=product[:], func=COPY, scale=weight)
-                        alone.append(weighted)
-                    elif in_sums < 2:
-                        nc.scalar.activation(out=sums[in_sums][:], in_=product[:], func=COPY, scale=weight)
-                        in_sums += 1
-                    else:
-                        running = sums[in_sums % 2]
-                        nc.vector.scalar_tensor_tensor(
-                            out=running[:], in0=product[:], scalar=weight, in1=running[:], op0=MULT, op1=ADD
-                        )
-                        in_sums += 1
-                for piece in turned_last_round:
-                    quantise(piece)
-                prepared = PREPARED_PER_ROUND[rounds % 2]
-                rounds += 1
-                turned_last_round, waiting = waiting[:prepared], waiting[prepared:]
-                spare = prepared - len(turned_last_round)
-                only_turned, waiting_late = waiting_late[:spare], waiting_late[spare:]
-                for piece in turned_last_round + only_turned:
-                    turn(piece, nc.scalar.copy)
-            parts.append(alone + [sums[in_sums % 2], sums[(in_sums - 1) % 2]])
+            for k in range(CONTEXTS):
+                terms.append((half, k, ctx_op, k, wc_ops[half], mean_weights[:, k : k + 1]))
+            terms.append((half, CONTEXTS, x_op, 0, wn_ops[half], 1.0))
+        sums = [[keep.tile([P, BANK], F32, name="sum%d_%d" % (g, c)) for c in range(2)] for g in range(HALVES)]
+        in_sums = [0, 0]
+        alone = [[], []]
+
+        def add_term(term):
+            half, index, stationary, block, moving, weight = term
+            product = product_pool.tile([P, BANK], F32, tag="product")
+            mx_pass(product, stationary, block, moving, True, True)
+            taken = in_sums[half]
+            if index in LEFT_TO_SCALAR[half]:
+                weighted = keep.tile([P, BANK], F32, name="weighted%d_%d" % (half, index))
+                nc.scalar.activation(out=weighted[:], in_=product[:], func=COPY, scale=weight)
+                alone[half].append(weighted)
+                return
+            running = sums[half][taken % 2]
+            if taken < 2:
+                nc.scalar.activation(out=running[:], in_=product[:], func=COPY, scale=weight)
+            else:
+                nc.vector.scalar_tensor_tensor(
+                    out=running[:], in0=product[:], scalar=weight, in1=running[:], op0=MULT, op1=ADD
+                )
+            in_sums[half] = taken + 1
 
         bias_columns = bias_rows[:].rearrange("r (g p t) -> r g t p", g=HALVES, t=PACK)
-        for half in range(HALVES):
+
+        def make_h(half):
+            last = (in_sums[half] - 1) % 2
+            parts = alone[half] + [sums[half][1 - last], sums[half][last]]
             h_turned = turned_pool.tile([P, PACK, P], F32, tag="turned")
             for t in range(PACK):
                 nc.tensor.matmul(
                     out=h_turned[:, t, :], lhsT=bias_columns[:, half, t, :], rhs=bias_weights_t[:],
                     start=(t == 0), stop=False,
                 )
-            for part in parts[half]:
+            for part in parts:
                 for t in range(PACK):
                     nc.tensor.matmul(
                         out=h_turned[:, t, :], lhsT=part[:, t * P : (t + 1) * P], rhs=identity_words[:],
-                        is_transpose=True, start=False, stop=(part is parts[half][-1] and t == PACK - 1),
+                        is_transpose=True, start=False, stop=(part is parts[-1] and t == PACK - 1),
                     )
             nc.scalar.copy(
                 out=h_ops[half]["grouped"][:].rearrange("p (r t) -> p r t", t=PACK),
                 in_=h_turned[:].rearrange("p t r -> p r t"),
             )
 
-        quantise(pairs_of(h_ops[0])[0])
+        bias_weights_t = keep.tile([P, P], BF16, name="bias_weights_t")
+        for r in range(ROUNDS):
+            run = pieces[done : done + RUNS[r]]
+            done += len(run)
+            for piece in run:
+                turn(piece, nc.scalar.copy)
+            if r == BIAS_ROUND:
+                bias_turned = turned_pool.tile([P, P], BF16, tag="turned")
+                nc.tensor.transpose(bias_turned[:], bias_weights[:], identity_values[:])
+                nc.scalar.copy(out=bias_weights_t[:], in_=bias_turned[:])
+            if r == H_ROUND:
+                make_h(0)
+                run.append(pairs_of(h_ops[0])[0])
+            late += run
+            for piece in late[:-1]:
+                quantise(piece)
+            late = late[-1:]
+            for i, term in enumerate(terms[r * ROUND : (r + 1) * ROUND]):
+                add_term(term)
+                if i == 0:
+                    for piece in late:
+                        quantise(piece)
+                    late = []
         out_sums = []
         for side in range(SIDES):
             out_sum = product_pool.tile([P, BANK], F32, tag="product")
             mx_pass(out_sum, h_ops[0], 0, wu_ops[0][side], True, False)
             out_sums.append(out_sum)
-        for side in range(SIDES):
-            for piece in pairs_of(wu_ops[1][side]):
-                quantise(piece)
+        make_h(1)
         quantise(pairs_of(h_ops[1])[0])
         result = keep.tile([P, F_OUT], F32, name="result")
         for side in range(SIDES):

@@ -27,13 +27,13 @@ SIDES = F_OUT // BANK
 
 GROUP = 4
 PAIR = 2
-ROUND = 5
 HEAD = 6
-ROUNDS = 7
-RUNS = (0, 3, 4, 3, 3, 3, 3)
+ROUNDS = 10
+RUNS = (1, 2, 2, 2, 2, 2, 2, 2, 2, 2)
+LATE_FROM = 8
 BIAS_ROUND = 3
-H_ROUND = 5
-LEFT_TO_SCALAR = ((11,), (11, 14))
+H_ROUND = 6
+LEFT_TO_SCALAR = ((11,),(11,14))
 
 FLOPS = 2 * (NODES * F_IN * HIDDEN + NODES * CONTEXTS * F_IN * HIDDEN + NODES * HIDDEN * F_OUT)
 
@@ -43,8 +43,8 @@ def tile_nodeembeddinglayer_pa_kernel(tc, x, contexts, attn, Wn, bn, Wc, bc, Wu,
     with ExitStack() as stack:
         stack.enter_context(tc.manual_schedule())
         keep = stack.enter_context(tc.tile_pool(name="keep", bufs=1))
-        turned_pool = stack.enter_context(tc.psum_pool(name="turned_pool", bufs=3))
-        product_pool = stack.enter_context(tc.psum_pool(name="product_pool", bufs=5))
+        turned_pool = stack.enter_context(tc.psum_pool(name="turned_pool", bufs=4))
+        product_pool = stack.enter_context(tc.psum_pool(name="product_pool", bufs=4))
 
         spark = keep.tile([P, 1], F32, name="spark")
         nc.vector.memset(spark[:], 0.0)
@@ -246,9 +246,10 @@ def tile_nodeembeddinglayer_pa_kernel(tc, x, contexts, attn, Wn, bn, Wc, bc, Wu,
             )
 
         bias_weights_t = keep.tile([P, P], BF16, name="bias_weights_t")
+        unquantised = []
         for r in range(ROUNDS):
             run = pieces[done : done + RUNS[r]]
-            done += len(run)
+            done += RUNS[r]
             for piece in run:
                 turn(piece, nc.scalar.copy)
             if r == BIAS_ROUND:
@@ -258,11 +259,14 @@ def tile_nodeembeddinglayer_pa_kernel(tc, x, contexts, attn, Wn, bn, Wc, bc, Wu,
             if r == H_ROUND:
                 make_h(0)
                 run.append(pairs_of(h_ops[0])[0])
+            if r >= LATE_FROM:
+                unquantised += run
+                run = []
             late += run
             for piece in late[:-1]:
                 quantise(piece)
             late = late[-1:]
-            for i, term in enumerate(terms[r * ROUND : (r + 1) * ROUND]):
+            for i, term in enumerate(terms[r * len(terms) // ROUNDS : (r + 1) * len(terms) // ROUNDS]):
                 add_term(term)
                 if i == 0:
                     for piece in late:
@@ -273,6 +277,8 @@ def tile_nodeembeddinglayer_pa_kernel(tc, x, contexts, attn, Wn, bn, Wc, bc, Wu,
             out_sum = product_pool.tile([P, BANK], F32, tag="product")
             mx_pass(out_sum, h_ops[0], 0, wu_ops[0][side], True, False)
             out_sums.append(out_sum)
+        for piece in unquantised:
+            quantise(piece)
         make_h(1)
         quantise(pairs_of(h_ops[1])[0])
         result = keep.tile([P, F_OUT], F32, name="result")

@@ -29,11 +29,11 @@ GROUP = 4
 PAIR = 2
 HEAD = 6
 ROUNDS = 10
-RUNS = (1, 2, 2, 2, 2, 2, 2, 2, 2, 2)
-LATE_FROM = 8
+RUNS = (2, 2, 3, 2, 2, 2, 2, 2, 2, 0)
+LATE_FROM = 7
 BIAS_ROUND = 3
-H_ROUND = 6
-LEFT_TO_SCALAR = ((11,),(11,14))
+H_ROUND = 7
+LEFT_TO_SCALAR = ((11,), (11, 14))
 
 FLOPS = 2 * (NODES * F_IN * HIDDEN + NODES * CONTEXTS * F_IN * HIDDEN + NODES * HIDDEN * F_OUT)
 
@@ -46,16 +46,9 @@ def tile_nodeembeddinglayer_pa_kernel(tc, x, contexts, attn, Wn, bn, Wc, bc, Wu,
         turned_pool = stack.enter_context(tc.psum_pool(name="turned_pool", bufs=4))
         product_pool = stack.enter_context(tc.psum_pool(name="product_pool", bufs=4))
 
-        spark = keep.tile([P, 1], F32, name="spark")
-        nc.vector.memset(spark[:], 0.0)
-        nc.scalar.activation(out=spark[:], in_=spark[:], func=COPY, scale=1.0)
-
         attn_raw = keep.tile([P, CONTEXTS], BF16, name="attn_raw")
         nc.scalar.dma_start(out=attn_raw[:], in_=attn)
         bias_rows = keep.tile([P, HIDDEN], BF16, name="bias_rows")
-        nc.vector.memset(bias_rows[:], 0.0)
-        nc.scalar.dma_start(out=bias_rows[0:CONTEXTS, :], in_=bc.partition_broadcast(CONTEXTS))
-        nc.scalar.dma_start(out=bias_rows[CONTEXTS : CONTEXTS + 1, :], in_=bn.unsqueeze(0))
 
         wc_raw = keep.tile([P, HALVES * GROUP * F_IN], BF16, name="wc_raw")
         wn_raw = keep.tile([P, HALVES * GROUP * F_IN], BF16, name="wn_raw")
@@ -63,6 +56,10 @@ def tile_nodeembeddinglayer_pa_kernel(tc, x, contexts, attn, Wn, bn, Wc, bc, Wu,
         x_raw = keep.tile([P, F_IN], BF16, name="x_raw")
         wu_raw = keep.tile([P, SIDES * GROUP * HIDDEN], BF16, name="wu_raw")
         bu_rows = keep.tile([P, F_OUT], BF16, name="bu_rows")
+
+        nc.vector.memset(bu_rows[:, 0:PAIR], 0.0)
+        nc.scalar.activation(out=bu_rows[:, 0:PAIR], in_=bu_rows[:, 0:PAIR], func=COPY, scale=1.0)
+        nc.vector.memset(bias_rows[:], 0.0)
 
         def load_hidden_rows(raw, weight, half):
             rows = weight.rearrange("(g p t) f -> g p (t f)", g=HALVES, t=PACK)[half]
@@ -94,6 +91,8 @@ def tile_nodeembeddinglayer_pa_kernel(tc, x, contexts, attn, Wn, bn, Wc, bc, Wu,
         load_hidden_rows(wn_raw, Wn, 1)
         for pair in range(SIDES * GROUP // PAIR):
             load_output_rows(pair)
+        nc.sync.dma_start(out=bias_rows[0:CONTEXTS, :], in_=bc.partition_broadcast(CONTEXTS))
+        nc.sync.dma_start(out=bias_rows[CONTEXTS : CONTEXTS + 1, :], in_=bn.unsqueeze(0))
         nc.sync.dma_start(out=bu_rows[:], in_=bu.partition_broadcast(P))
 
         identity_words = keep.tile([P, P], F32, name="identity_words")
@@ -176,11 +175,9 @@ def tile_nodeembeddinglayer_pa_kernel(tc, x, contexts, attn, Wn, bn, Wc, bc, Wu,
         ]
 
         mean_weights = keep.tile([P, CONTEXTS], F32, name="mean_weights")
-        nc.scalar.activation(out=mean_weights[:], in_=attn_raw[:], func=COPY, scale=1.0 / CONTEXTS)
         bias_weights = keep.tile([P, P], BF16, name="bias_weights")
         nc.vector.memset(bias_weights[:], 0.0)
         nc.vector.memset(bias_weights[:, CONTEXTS : CONTEXTS + 1], 1.0)
-        nc.vector.tensor_copy(out=bias_weights[:, 0:CONTEXTS], in_=mean_weights[:])
 
         pieces = (
             pairs_of(wc_ops[0]) + pairs_of(ctx_op) + pairs_of(x_op) + pairs_of(wn_ops[0]) + pairs_of(wc_ops[1])
@@ -192,8 +189,11 @@ def tile_nodeembeddinglayer_pa_kernel(tc, x, contexts, attn, Wn, bn, Wc, bc, Wu,
             turn(pieces[i], nc.vector.tensor_copy if i % 3 == 1 else nc.scalar.copy)
             if i > 0:
                 quantise(pieces[i - 1])
-        late = [pieces[HEAD - 1]]
+        quantise(pieces[HEAD - 1])
         done = HEAD
+
+        nc.scalar.activation(out=mean_weights[:], in_=attn_raw[:], func=COPY, scale=1.0 / CONTEXTS)
+        nc.vector.tensor_copy(out=bias_weights[:, 0:CONTEXTS], in_=mean_weights[:])
 
         terms = []
         for half in range(HALVES):
@@ -256,22 +256,16 @@ def tile_nodeembeddinglayer_pa_kernel(tc, x, contexts, attn, Wn, bn, Wc, bc, Wu,
                 bias_turned = turned_pool.tile([P, P], BF16, tag="turned")
                 nc.tensor.transpose(bias_turned[:], bias_weights[:], identity_values[:])
                 nc.scalar.copy(out=bias_weights_t[:], in_=bias_turned[:])
-            if r == H_ROUND:
-                make_h(0)
-                run.append(pairs_of(h_ops[0])[0])
             if r >= LATE_FROM:
                 unquantised += run
                 run = []
-            late += run
-            for piece in late[:-1]:
-                quantise(piece)
-            late = late[-1:]
-            for i, term in enumerate(terms[r * len(terms) // ROUNDS : (r + 1) * len(terms) // ROUNDS]):
+            if r == H_ROUND:
+                make_h(0)
+                run = run + pairs_of(h_ops[0])
+            for term in terms[r * len(terms) // ROUNDS : (r + 1) * len(terms) // ROUNDS]:
                 add_term(term)
-                if i == 0:
-                    for piece in late:
-                        quantise(piece)
-                    late = []
+            for piece in run:
+                quantise(piece)
         out_sums = []
         for side in range(SIDES):
             out_sum = product_pool.tile([P, BANK], F32, tag="product")

@@ -27,13 +27,14 @@ SIDES = F_OUT // BANK
 
 GROUP = 4
 PAIR = 2
-HEAD = 6
+HEAD = 5
 ROUNDS = 10
-RUNS = (2, 2, 3, 2, 2, 2, 2, 2, 2, 0)
-LATE_FROM = 7
+RUNS = (1, 2, 2, 3, 3, 2, 2, 2, 2, 1)
+LATE_FROM = 8
+PRODUCTS = (3, 3, 4, 3, 4, 3, 4, 3, 4, 3)
 BIAS_ROUND = 3
 H_ROUND = 7
-LEFT_TO_SCALAR = ((11,), (11, 14))
+LEFT_TO_SCALAR = ((3, 7, 11), (3, 7, 11))
 
 FLOPS = 2 * (NODES * F_IN * HIDDEN + NODES * CONTEXTS * F_IN * HIDDEN + NODES * HIDDEN * F_OUT)
 
@@ -179,6 +180,13 @@ def tile_nodeembeddinglayer_pa_kernel(tc, x, contexts, attn, Wn, bn, Wc, bc, Wu,
         nc.vector.memset(bias_weights[:], 0.0)
         nc.vector.memset(bias_weights[:, CONTEXTS : CONTEXTS + 1], 1.0)
 
+        def quantise_group(piece):
+            operand, first, count = piece
+            if operand["blocks"] < GROUP:
+                quantise(piece)
+            elif first % GROUP:
+                quantise((operand, first - count, GROUP))
+
         pieces = (
             pairs_of(wc_ops[0]) + pairs_of(ctx_op) + pairs_of(x_op) + pairs_of(wn_ops[0]) + pairs_of(wc_ops[1])
             + pairs_of(wn_ops[1]) + pairs_of(wu_ops[0][0]) + pairs_of(wu_ops[0][1]) + pairs_of(wu_ops[1][0])
@@ -186,7 +194,7 @@ def tile_nodeembeddinglayer_pa_kernel(tc, x, contexts, attn, Wn, bn, Wc, bc, Wu,
         )
 
         for i in range(HEAD):
-            turn(pieces[i], nc.vector.tensor_copy if i % 3 == 1 else nc.scalar.copy)
+            turn(pieces[i], nc.vector.tensor_copy if i % 3 in (1,) else nc.scalar.copy)
             if i > 0:
                 quantise(pieces[i - 1])
         quantise(pieces[HEAD - 1])
@@ -212,10 +220,15 @@ def tile_nodeembeddinglayer_pa_kernel(tc, x, contexts, attn, Wn, bn, Wc, bc, Wu,
             if index in LEFT_TO_SCALAR[half]:
                 weighted = keep.tile([P, BANK], F32, name="weighted%d_%d" % (half, index))
                 nc.scalar.activation(out=weighted[:], in_=product[:], func=COPY, scale=weight)
-                alone[half].append(weighted)
+                if alone[half]:
+                    nc.gpsimd.tensor_add(out=alone[half][0][:], in0=alone[half][0][:], in1=weighted[:])
+                else:
+                    alone[half].append(weighted)
                 return
             running = sums[half][taken % 2]
-            if taken < 2:
+            if half == 0 and taken == 0:
+                nc.vector.tensor_scalar_mul(out=running[:], in0=product[:], scalar1=weight)
+            elif taken < 2:
                 nc.scalar.activation(out=running[:], in_=product[:], func=COPY, scale=weight)
             else:
                 nc.vector.scalar_tensor_tensor(
@@ -262,18 +275,20 @@ def tile_nodeembeddinglayer_pa_kernel(tc, x, contexts, attn, Wn, bn, Wc, bc, Wu,
             if r == H_ROUND:
                 make_h(0)
                 run = run + pairs_of(h_ops[0])
-            for term in terms[r * len(terms) // ROUNDS : (r + 1) * len(terms) // ROUNDS]:
+            this_round = terms[sum(PRODUCTS[:r]) : sum(PRODUCTS[: r + 1])]
+            for term in this_round:
                 add_term(term)
-            for piece in run:
-                quantise(piece)
+                if term is this_round[min(2, len(this_round)) - 1]:
+                    for piece in run:
+                        quantise_group(piece)
+        make_h(1)
+        for piece in unquantised:
+            quantise_group(piece)
         out_sums = []
         for side in range(SIDES):
             out_sum = product_pool.tile([P, BANK], F32, tag="product")
             mx_pass(out_sum, h_ops[0], 0, wu_ops[0][side], True, False)
             out_sums.append(out_sum)
-        for piece in unquantised:
-            quantise(piece)
-        make_h(1)
         quantise(pairs_of(h_ops[1])[0])
         result = keep.tile([P, F_OUT], F32, name="result")
         for side in range(SIDES):

@@ -27,14 +27,13 @@ SIDES = F_OUT // BANK
 
 GROUP = 4
 PAIR = 2
-HEAD = 5
-ROUNDS = 10
-RUNS = (1, 2, 2, 3, 3, 2, 2, 2, 2, 1)
-LATE_FROM = 8
-PRODUCTS = (3, 3, 4, 3, 4, 3, 4, 3, 4, 3)
+HEAD = 4
+ROUNDS = 9
+RUNS = (2, 3, 3, 3, 2, 2, 2, 2, 2)
+LATE_FROM = 7
 BIAS_ROUND = 3
 H_ROUND = 7
-LEFT_TO_SCALAR = ((3, 7, 11), (3, 7, 11))
+LEFT_TO_SCALAR = ((4, 8, 12), (4, 8, 12))
 
 FLOPS = 2 * (NODES * F_IN * HIDDEN + NODES * CONTEXTS * F_IN * HIDDEN + NODES * HIDDEN * F_OUT)
 
@@ -240,7 +239,7 @@ def tile_nodeembeddinglayer_pa_kernel(tc, x, contexts, attn, Wn, bn, Wc, bc, Wu,
 
         def make_h(half):
             last = (in_sums[half] - 1) % 2
-            parts = alone[half] + [sums[half][1 - last], sums[half][last]]
+            parts = alone[half] + ([sums[half][1 - last], sums[half][last]] if half else [])
             h_turned = turned_pool.tile([P, PACK, P], F32, tag="turned")
             for t in range(PACK):
                 nc.tensor.matmul(
@@ -275,7 +274,10 @@ def tile_nodeembeddinglayer_pa_kernel(tc, x, contexts, attn, Wn, bn, Wc, bc, Wu,
             if r == H_ROUND:
                 make_h(0)
                 run = run + pairs_of(h_ops[0])
-            this_round = terms[sum(PRODUCTS[:r]) : sum(PRODUCTS[: r + 1])]
+            if r == H_ROUND - 1:
+                for part in sums[0]:
+                    nc.gpsimd.tensor_add(out=alone[0][0][:], in0=alone[0][0][:], in1=part[:])
+            this_round = terms[r * len(terms) // ROUNDS : (r + 1) * len(terms) // ROUNDS]
             for term in this_round:
                 add_term(term)
                 if term is this_round[min(2, len(this_round)) - 1]:

@@ -28,9 +28,9 @@ SIDES = F_OUT // BANK
 GROUP = 4
 PAIR = 2
 HEAD = 4
-ROUNDS = 9
-RUNS = (2, 3, 3, 3, 2, 2, 2, 2, 2)
-LATE_FROM = 7
+RUNS = (2, 2, 3, 2, 2, 2, 2, 1, 1, 2, 2)
+PRODUCTS = (3, 3, 3, 3, 3, 4, 4, 4, 4, 3, 0)
+LATE_FROM = 9
 BIAS_ROUND = 3
 H_ROUND = 7
 LEFT_TO_SCALAR = ((4, 8, 12), (4, 8, 12))
@@ -61,36 +61,35 @@ def tile_nodeembeddinglayer_pa_kernel(tc, x, contexts, attn, Wn, bn, Wc, bc, Wu,
         nc.scalar.activation(out=bu_rows[:, 0:PAIR], in_=bu_rows[:, 0:PAIR], func=COPY, scale=1.0)
         nc.vector.memset(bias_rows[:], 0.0)
 
-        def load_hidden_rows(raw, weight, half):
+        def load_hidden_rows(raw, weight, half, loads):
             rows = weight.rearrange("(g p t) f -> g p (t f)", g=HALVES, t=PACK)[half]
-            for u in range(2):
-                pair = half * 2 + u
+            for first, last in loads:
                 nc.sync.dma_start(
-                    out=raw[:, pair * PAIR * F_IN : (pair + 1) * PAIR * F_IN],
-                    in_=rows[:, u * PAIR * F_IN : (u + 1) * PAIR * F_IN],
+                    out=raw[:, (half * PACK + first) * F_IN : (half * PACK + last) * F_IN],
+                    in_=rows[:, first * F_IN : last * F_IN],
                 )
 
-        def load_contexts(pair):
-            columns = slice(pair * PAIR * F_IN, (pair + 1) * PAIR * F_IN)
+        def load_contexts(first, blocks):
+            columns = slice(first * F_IN, (first + blocks) * F_IN)
             nc.sync.dma_start(out=ctx_raw[:, columns], in_=contexts.rearrange("n k f -> n (k f)")[:, columns])
 
-        def load_output_rows(pair):
+        def load_output_rows(side):
             nc.sync.dma_start(
-                out=wu_raw[:, pair * PAIR * HIDDEN : (pair + 1) * PAIR * HIDDEN].rearrange(
-                    "p (b h) -> p b h", b=PAIR
-                ),
-                in_=Wu.rearrange("(b p) h -> p b h", p=P)[:, pair * PAIR : (pair + 1) * PAIR, :],
+                out=wu_raw[:, side * GROUP * HIDDEN : (side + 1) * GROUP * HIDDEN],
+                in_=Wu.rearrange("(g p b) h -> g p (b h)", g=SIDES, b=GROUP)[side],
             )
 
-        load_hidden_rows(wc_raw, Wc, 0)
-        for pair in range(CONTEXTS // PAIR):
-            load_contexts(pair)
+        load_hidden_rows(wc_raw, Wc, 0, ((0, 1), (1, 2), (2, 4)))
+        for first in range(0, CONTEXTS // 2, PAIR):
+            load_contexts(first, PAIR)
+        for first in range(CONTEXTS // 2, CONTEXTS, GROUP):
+            load_contexts(first, GROUP)
         nc.sync.dma_start(out=x_raw[:], in_=x)
-        load_hidden_rows(wn_raw, Wn, 0)
-        load_hidden_rows(wc_raw, Wc, 1)
-        load_hidden_rows(wn_raw, Wn, 1)
-        for pair in range(SIDES * GROUP // PAIR):
-            load_output_rows(pair)
+        load_hidden_rows(wn_raw, Wn, 0, ((0, PACK),))
+        load_hidden_rows(wc_raw, Wc, 1, ((0, PACK),))
+        load_hidden_rows(wn_raw, Wn, 1, ((0, PACK),))
+        for side in range(SIDES):
+            load_output_rows(side)
         nc.sync.dma_start(out=bias_rows[0:CONTEXTS, :], in_=bc.partition_broadcast(CONTEXTS))
         nc.sync.dma_start(out=bias_rows[CONTEXTS : CONTEXTS + 1, :], in_=bn.unsqueeze(0))
         nc.sync.dma_start(out=bu_rows[:], in_=bu.partition_broadcast(P))
@@ -239,7 +238,7 @@ def tile_nodeembeddinglayer_pa_kernel(tc, x, contexts, attn, Wn, bn, Wc, bc, Wu,
 
         def make_h(half):
             last = (in_sums[half] - 1) % 2
-            parts = alone[half] + ([sums[half][1 - last], sums[half][last]] if half else [])
+            parts = [sums[half][1 - last], alone[half][0], sums[half][last]] if half else alone[half]
             h_turned = turned_pool.tile([P, PACK, P], F32, tag="turned")
             for t in range(PACK):
                 nc.tensor.matmul(
@@ -259,7 +258,7 @@ def tile_nodeembeddinglayer_pa_kernel(tc, x, contexts, attn, Wn, bn, Wc, bc, Wu,
 
         bias_weights_t = keep.tile([P, P], BF16, name="bias_weights_t")
         unquantised = []
-        for r in range(ROUNDS):
+        for r in range(len(RUNS)):
             run = pieces[done : done + RUNS[r]]
             done += RUNS[r]
             for piece in run:
@@ -277,7 +276,7 @@ def tile_nodeembeddinglayer_pa_kernel(tc, x, contexts, attn, Wn, bn, Wc, bc, Wu,
             if r == H_ROUND - 1:
                 for part in sums[0]:
                     nc.gpsimd.tensor_add(out=alone[0][0][:], in0=alone[0][0][:], in1=part[:])
-            this_round = terms[r * len(terms) // ROUNDS : (r + 1) * len(terms) // ROUNDS]
+            this_round = terms[sum(PRODUCTS[:r]) : sum(PRODUCTS[: r + 1])]
             for term in this_round:
                 add_term(term)
                 if term is this_round[min(2, len(this_round)) - 1]:
@@ -296,5 +295,9 @@ def tile_nodeembeddinglayer_pa_kernel(tc, x, contexts, attn, Wn, bn, Wc, bc, Wu,
         for side in range(SIDES):
             columns = slice(side * BANK, (side + 1) * BANK)
             mx_pass(out_sums[side], h_ops[1], 0, wu_ops[1][side], False, True)
-            nc.vector.tensor_add(out=result[:, columns], in0=out_sums[side][:], in1=bu_rows[:, columns])
+            nc.vector.tensor_add(
+                out=result[:, columns].rearrange("n (r b) -> n r b", b=GROUP),
+                in0=out_sums[side][:].rearrange("n (b r) -> n r b", b=GROUP),
+                in1=bu_rows[:, columns].rearrange("n (r b) -> n r b", b=GROUP),
+            )
             nc.sync.dma_start(out=out[:, columns], in_=result[:, columns])

from contextlib import ExitStack

import concourse.mybir as mybir
from concourse.masks import make_identity

F32 = mybir.dt.float32
BF16 = mybir.dt.bfloat16
U32 = mybir.dt.uint32
U8 = mybir.dt.uint8
FP8X4 = mybir.dt.float8_e4m3fn_x4
MULT = mybir.AluOpType.mult
ADD = mybir.AluOpType.add
COPY = mybir.ActivationFunctionType.Copy

P = 128
PACK = 4
K_PASS = P * PACK
BANK = 512

NODES = 128
CONTEXTS = 16
F_IN = 512
HIDDEN = 1024
F_OUT = 1024
HALVES = HIDDEN // K_PASS
SIDES = F_OUT // BANK

GROUP = 4
PAIR = 2
HEAD = 4
RUNS = (2, 2, 3, 2, 2, 2, 2, 1, 1, 2, 2)
PRODUCTS = (3, 3, 3, 3, 3, 4, 4, 4, 4, 3, 0)
LATE_FROM = 9
BIAS_ROUND = 3
H_ROUND = 7
LEFT_TO_SCALAR = ((4, 8, 12), (4, 8, 12))

FLOPS = 2 * (NODES * F_IN * HIDDEN + NODES * CONTEXTS * F_IN * HIDDEN + NODES * HIDDEN * F_OUT)


def tile_nodeembeddinglayer_pa_kernel(tc, x, contexts, attn, Wn, bn, Wc, bc, Wu, bu, out):
    nc = tc.nc
    with ExitStack() as stack:
        stack.enter_context(tc.manual_schedule())
        keep = stack.enter_context(tc.tile_pool(name="keep", bufs=1))
        turned_pool = stack.enter_context(tc.psum_pool(name="turned_pool", bufs=4))
        product_pool = stack.enter_context(tc.psum_pool(name="product_pool", bufs=4))

        attn_raw = keep.tile([P, CONTEXTS], BF16, name="attn_raw")
        nc.scalar.dma_start(out=attn_raw[:], in_=attn)
        bias_rows = keep.tile([P, HIDDEN], BF16, name="bias_rows")

        wc_raw = keep.tile([P, HALVES * GROUP * F_IN], BF16, name="wc_raw")
        wn_raw = keep.tile([P, HALVES * GROUP * F_IN], BF16, name="wn_raw")
        ctx_raw = keep.tile([P, CONTEXTS * F_IN], BF16, name="ctx_raw")
        x_raw = keep.tile([P, F_IN], BF16, name="x_raw")
        wu_raw = keep.tile([P, SIDES * GROUP * HIDDEN], BF16, name="wu_raw")
        bu_rows = keep.tile([P, F_OUT], BF16, name="bu_rows")

        nc.vector.memset(bu_rows[:, 0:PAIR], 0.0)
        nc.scalar.activation(out=bu_rows[:, 0:PAIR], in_=bu_rows[:, 0:PAIR], func=COPY, scale=1.0)
        nc.vector.memset(bias_rows[:], 0.0)

        def load_hidden_rows(raw, weight, half, loads):
            rows = weight.rearrange("(g p t) f -> g p (t f)", g=HALVES, t=PACK)[half]
            for first, last in loads:
                nc.sync.dma_start(
                    out=raw[:, (half * PACK + first) * F_IN : (half * PACK + last) * F_IN],
                    in_=rows[:, first * F_IN : last * F_IN],
                )

        def load_contexts(first, blocks):
            columns = slice(first * F_IN, (first + blocks) * F_IN)
            nc.sync.dma_start(out=ctx_raw[:, columns], in_=contexts.rearrange("n k f -> n (k f)")[:, columns])

        def load_output_rows(side):
            nc.sync.dma_start(
                out=wu_raw[:, side * GROUP * HIDDEN : (side + 1) * GROUP * HIDDEN],
                in_=Wu.rearrange("(g p b) h -> g p (b h)", g=SIDES, b=GROUP)[side],
            )

        load_hidden_rows(wc_raw, Wc, 0, ((0, 1), (1, 2), (2, 4)))
        for first in range(0, CONTEXTS // 2, PAIR):
            load_contexts(first, PAIR)
        for first in range(CONTEXTS // 2, CONTEXTS, GROUP):
            load_contexts(first, GROUP)
        nc.sync.dma_start(out=x_raw[:], in_=x)
        load_hidden_rows(wn_raw, Wn, 0, ((0, PACK),))
        load_hidden_rows(wc_raw, Wc, 1, ((0, PACK),))
        load_hidden_rows(wn_raw, Wn, 1, ((0, PACK),))
        for side in range(SIDES):
            load_output_rows(side)
        nc.sync.dma_start(out=bias_rows[0:CONTEXTS, :], in_=bc.partition_broadcast(CONTEXTS))
        nc.sync.dma_start(out=bias_rows[CONTEXTS : CONTEXTS + 1, :], in_=bn.unsqueeze(0))
        nc.sync.dma_start(out=bu_rows[:], in_=bu.partition_broadcast(P))

        identity_words = keep.tile([P, P], F32, name="identity_words")
        make_identity(nc, identity_words[:])
        identity_values = keep.tile([P, P], BF16, name="identity_values")
        make_identity(nc, identity_values[:])

        def new_operand(name, blocks, source):
            columns = blocks * P
            return {
                "blocks": blocks,
                "source": source,
                "grouped": keep.tile([P, columns * PACK], BF16, name=name + "_grouped", align_bytes=64),
                "codes": keep.tile([P, columns], U32, name=name + "_codes", align_bytes=64),
                "scales": keep.tile([P, columns], U8, name=name + "_scales", align_bytes=64),
            }

        def pairs_of(operand):
            step = min(operand["blocks"], PAIR)
            return [(operand, first, step) for first in range(0, operand["blocks"], step)]

        def words(raw, blocks):
            return raw[:].bitcast(F32).rearrange("p (b w) -> p b w", b=blocks)

        def turn(piece, copy_out):
            operand, first, count = piece
            turned = turned_pool.tile([P, count, 2, P], F32, tag="turned")
            for i in range(count):
                for u in range(2):
                    nc.tensor.transpose(
                        turned[:, i, u, :], operand["source"][:, first + i, u : 2 * P : 2], identity_words[:]
                    )
            copy_out(
                out=operand["grouped"][:].bitcast(F32)[:, first * P * 2 : (first + count) * P * 2].rearrange(
                    "p (i r u) -> p i r u", i=count, u=2
                ),
                in_=turned[:].rearrange("p i u r -> p i r u"),
            )

        def quantise(piece):
            operand, first, count = piece
            columns = slice(first * P, (first + count) * P)
            nc.vector.quantize_mx(
                out=operand["codes"][:, columns].bitcast(FP8X4),
                scales=operand["scales"][:, columns],
                in_=operand["grouped"][:, first * P * PACK : (first + count) * P * PACK],
            )

        def mx_pass(acc, stationary, block, moving, start, stop):
            columns = slice(block * P, (block + 1) * P)
            nc.tensor.matmul_mx(
                out=acc[:],
                lhsT=stationary["codes"][:, columns].bitcast(FP8X4),
                lhsT_scale=stationary["scales"][:, columns],
                rhs=moving["codes"][:].bitcast(FP8X4),
                rhs_scale=moving["scales"][:],
                start=start,
                stop=stop,
            )

        wc_words = words(wc_raw, HALVES * GROUP)
        wn_words = words(wn_raw, HALVES * GROUP)
        wu_words = words(wu_raw, SIDES * GROUP)

        ctx_op = new_operand("ctx", CONTEXTS, words(ctx_raw, CONTEXTS))
        x_op = new_operand("x", 1, words(x_raw, 1))
        wc_ops = [new_operand("wc%d" % g, GROUP, wc_words[:, g * GROUP : (g + 1) * GROUP, :]) for g in range(HALVES)]
        wn_ops = [new_operand("wn%d" % g, GROUP, wn_words[:, g * GROUP : (g + 1) * GROUP, :]) for g in range(HALVES)]
        h_ops = [new_operand("h%d" % g, 1, None) for g in range(HALVES)]
        wu_ops = [
            [
                new_operand(
                    "wu%d%d" % (g, side),
                    GROUP,
                    wu_words[:, side * GROUP : (side + 1) * GROUP, g * K_PASS // 2 : (g + 1) * K_PASS // 2],
                )
                for side in range(SIDES)
            ]
            for g in range(HALVES)
        ]

        mean_weights = keep.tile([P, CONTEXTS], F32, name="mean_weights")
        bias_weights = keep.tile([P, P], BF16, name="bias_weights")
        nc.vector.memset(bias_weights[:], 0.0)
        nc.vector.memset(bias_weights[:, CONTEXTS : CONTEXTS + 1], 1.0)

        def quantise_group(piece):
            operand, first, count = piece
            if operand["blocks"] < GROUP:
                quantise(piece)
            elif first % GROUP:
                quantise((operand, first - count, GROUP))

        pieces = (
            pairs_of(wc_ops[0]) + pairs_of(ctx_op) + pairs_of(x_op) + pairs_of(wn_ops[0]) + pairs_of(wc_ops[1])
            + pairs_of(wn_ops[1]) + pairs_of(wu_ops[0][0]) + pairs_of(wu_ops[0][1]) + pairs_of(wu_ops[1][0])
            + pairs_of(wu_ops[1][1])
        )

        for i in range(HEAD):
            turn(pieces[i], nc.vector.tensor_copy if i % 3 in (1,) else nc.scalar.copy)
            if i > 0:
                quantise(pieces[i - 1])
        quantise(pieces[HEAD - 1])
        done = HEAD

        nc.scalar.activation(out=mean_weights[:], in_=attn_raw[:], func=COPY, scale=1.0 / CONTEXTS)
        nc.vector.tensor_copy(out=bias_weights[:, 0:CONTEXTS], in_=mean_weights[:])

        terms = []
        for half in range(HALVES):
            for k in range(CONTEXTS):
                terms.append((half, k, ctx_op, k, wc_ops[half], mean_weights[:, k : k + 1]))
            terms.append((half, CONTEXTS, x_op, 0, wn_ops[half], 1.0))
        sums = [[keep.tile([P, BANK], F32, name="sum%d_%d" % (g, c)) for c in range(2)] for g in range(HALVES)]
        in_sums = [0, 0]
        alone = [[], []]

        def add_term(term):
            half, index, stationary, block, moving, weight = term
            product = product_pool.tile([P, BANK], F32, tag="product")
            mx_pass(product, stationary, block, moving, True, True)
            taken = in_sums[half]
            if index in LEFT_TO_SCALAR[half]:
                weighted = keep.tile([P, BANK], F32, name="weighted%d_%d" % (half, index))
                nc.scalar.activation(out=weighted[:], in_=product[:], func=COPY, scale=weight)
                if alone[half]:
                    nc.gpsimd.tensor_add(out=alone[half][0][:], in0=alone[half][0][:], in1=weighted[:])
                else:
                    alone[half].append(weighted)
                return
            running = sums[half][taken % 2]
            if half == 0 and taken == 0:
                nc.vector.tensor_scalar_mul(out=running[:], in0=product[:], scalar1=weight)
            elif taken < 2:
                nc.scalar.activation(out=running[:], in_=product[:], func=COPY, scale=weight)
            else:
                nc.vector.scalar_tensor_tensor(
                    out=running[:], in0=product[:], scalar=weight, in1=running[:], op0=MULT, op1=ADD
                )
            in_sums[half] = taken + 1

        bias_columns = bias_rows[:].rearrange("r (g p t) -> r g t p", g=HALVES, t=PACK)

        def make_h(half):
            last = (in_sums[half] - 1) % 2
            parts = [sums[half][1 - last], alone[half][0], sums[half][last]] if half else alone[half]
            h_turned = turned_pool.tile([P, PACK, P], F32, tag="turned")
            for t in range(PACK):
                nc.tensor.matmul(
                    out=h_turned[:, t, :], lhsT=bias_columns[:, half, t, :], rhs=bias_weights_t[:],
                    start=(t == 0), stop=False,
                )
            for part in parts:
                for t in range(PACK):
                    nc.tensor.matmul(
                        out=h_turned[:, t, :], lhsT=part[:, t * P : (t + 1) * P], rhs=identity_words[:],
                        is_transpose=True, start=False, stop=(part is parts[-1] and t == PACK - 1),
                    )
            nc.scalar.copy(
                out=h_ops[half]["grouped"][:].rearrange("p (r t) -> p r t", t=PACK),
                in_=h_turned[:].rearrange("p t r -> p r t"),
            )

        bias_weights_t = keep.tile([P, P], BF16, name="bias_weights_t")
        unquantised = []
        for r in range(len(RUNS)):
            run = pieces[done : done + RUNS[r]]
            done += RUNS[r]
            for piece in run:
                turn(piece, nc.scalar.copy)
            if r == BIAS_ROUND:
                bias_turned = turned_pool.tile([P, P], BF16, tag="turned")
                nc.tensor.transpose(bias_turned[:], bias_weights[:], identity_values[:])
                nc.scalar.copy(out=bias_weights_t[:], in_=bias_turned[:])
            if r >= LATE_FROM:
                unquantised += run
                run = []
            if r == H_ROUND:
                make_h(0)
                run = run + pairs_of(h_ops[0])
            if r == H_ROUND - 1:
                for part in sums[0]:
                    nc.gpsimd.tensor_add(out=alone[0][0][:], in0=alone[0][0][:], in1=part[:])
            this_round = terms[sum(PRODUCTS[:r]) : sum(PRODUCTS[: r + 1])]
            for term in this_round:
                add_term(term)
                if term is this_round[min(2, len(this_round)) - 1]:
                    for piece in run:
                        quantise_group(piece)
        make_h(1)
        for piece in unquantised:
            quantise_group(piece)
        out_sums = []
        for side in range(SIDES):
            out_sum = product_pool.tile([P, BANK], F32, tag="product")
            mx_pass(out_sum, h_ops[0], 0, wu_ops[0][side], True, False)
            out_sums.append(out_sum)
        quantise(pairs_of(h_ops[1])[0])
        result = keep.tile([P, F_OUT], F32, name="result")
        for side in range(SIDES):
            columns = slice(side * BANK, (side + 1) * BANK)
            mx_pass(out_sums[side], h_ops[1], 0, wu_ops[1][side], False, True)
            nc.vector.tensor_add(
                out=result[:, columns].rearrange("n (r b) -> n r b", b=GROUP),
                in0=out_sums[side][:].rearrange("n (b r) -> n r b", b=GROUP),
                in1=bu_rows[:, columns].rearrange("n (r b) -> n r b", b=GROUP),
            )
            nc.sync.dma_start(out=out[:, columns], in_=result[:, columns])
